import numpy as np
import ml_dtypes


def mxq(x, axis, fmt="e4m3"):
    dtype, down = {"e4m3": (ml_dtypes.float8_e4m3fn, 7), "e5m2": (ml_dtypes.float8_e5m2, 14)}[fmt]
    v = np.moveaxis(np.asarray(x, np.float32).astype(ml_dtypes.bfloat16).astype(np.float64), axis, -1)
    blocks = v.reshape(v.shape[:-1] + (-1, 32))
    amax = np.abs(blocks).max(-1, keepdims=True)
    byte = np.maximum(np.where(amax > 0, np.frexp(amax)[1] - 1 + 127, 0) - down, 1)
    scale = np.exp2(byte - 127.0)
    codes = (blocks / scale).astype(np.float32).astype(dtype).astype(np.float64)
    return np.moveaxis((codes * scale).reshape(v.shape), -1, axis)


WIDE = False


def mx_kscale(k):
    if not WIDE:
        return np.ones(k)
    levels = np.array([10, -10, 5, -5, 0])
    a = np.random.permutation(np.resize(levels, k // 512 * 4)).reshape(k // 512, 4)
    idx = np.arange(k)
    return np.exp2(a[idx // 512, idx % 128 // 32])


BF16 = ml_dtypes.bfloat16


def bf(x):
    return np.asarray(x, np.float32).astype(BF16)


def f64(x):
    return np.asarray(x).astype(np.float64)


B, I, O, G = 8192, 128, 512, 8


def setup_inputs():
    s = mx_kscale(I * G).reshape(I, G)[:, 0]
    a = np.log2(s / s.max())
    d = np.sqrt(np.abs(a) * np.log(2.0) / 20.0)
    u = np.random.random((B, I))
    x = np.where(a < 0, 1.0 + d + 0.1 * (u - 0.5), u)
    w = np.random.standard_normal((I * G, O)) * 2.0 / np.sqrt(I * G) * np.repeat(np.exp2(-a), G)[:, None]
    return {"x": bf(x), "spline_weight": bf(w), "base_weight": bf(np.random.standard_normal((O, I)) / np.sqrt(I)),
            "grid": bf(np.linspace(0.0, 1.0, G))}


def reference(x, spline_weight, base_weight, grid):
    x = f64(x)
    base_output = x @ f64(base_weight).T
    basis = np.exp(-20.0 * (x[:, :, None] - f64(grid)[None, None, :]) ** 2)
    basis = basis.reshape(x.shape[0], -1)
    return base_output + (mxq(basis, 1, "e4m3") @ mxq(f64(spline_weight), 0, "e4m3"))

@@ -1,0 +1,195 @@
+from contextlib import ExitStack
+
+import concourse.mybir as mybir
+from concourse.masks import make_identity
+
+F32 = mybir.dt.float32
+BF16 = mybir.dt.bfloat16
+U32 = mybir.dt.uint32
+U8 = mybir.dt.uint8
+FP8X4 = mybir.dt.float8_e4m3fn_x4
+ACT = mybir.ActivationFunctionType
+ALU = mybir.AluOpType
+
+P = 128
+BATCH = 8192
+FEAT = 128
+OUTS = 512
+GRID = 8
+NJ = BATCH // P
+CH = 1024
+JCH = CH // P
+N_CH = BATCH // CH
+JRES = 4
+FLOPS = 2 * BATCH * (FEAT * GRID) * OUTS + 2 * BATCH * FEAT * OUTS
+
+POOL_STAGES = (2, 5, 7, 10, 13, 15)
+X_LOADS = ((0, 8), (8, 24), (24, 64))
+
+
+def tile_rbfkanlayer_t_kernel(tc, x, spline_weight, base_weight, grid, out):
+    nc = tc.nc
+    with ExitStack() as stack:
+        keep = stack.enter_context(tc.tile_pool(name="keep", bufs=1))
+        sqa = stack.enter_context(tc.tile_pool(name="sqa", bufs=2))
+        sqp = stack.enter_context(tc.tile_pool(name="sqp", bufs=2))
+        gp = stack.enter_context(tc.tile_pool(name="gp", bufs=2))
+        cp = stack.enter_context(tc.tile_pool(name="cp", bufs=4))
+        rp = stack.enter_context(tc.tile_pool(name="rp", bufs=4))
+        ps_a = stack.enter_context(tc.psum_pool(name="ps_a", bufs=4))
+        ps_m = stack.enter_context(tc.psum_pool(name="ps_m", bufs=4))
+
+        gb = keep.tile([P, GRID], BF16)
+        nc.scalar.dma_start(out=gb[:], in_=grid.partition_broadcast(P))
+        xin = keep.tile([P, NJ * FEAT], BF16)
+        x_view = x.rearrange("(p j) i -> p (j i)", j=NJ)
+
+        def load_x(j0, j1):
+            nc.sync.dma_start(out=xin[:, j0 * FEAT : j1 * FEAT], in_=x_view[:, j0 * FEAT : j1 * FEAT])
+
+        load_x(*X_LOADS[0])
+        wraw = keep.tile([P, GRID, OUTS], BF16)
+        nc.sync.dma_start(
+            out=wraw[:].rearrange("p g o -> p (g o)"),
+            in_=spline_weight.rearrange("(i g) o -> i (g o)", g=GRID),
+        )
+        bwin = keep.tile([P, 4 * FEAT], BF16)
+        nc.sync.dma_start(
+            out=bwin[:].rearrange("p (t i) -> p t i", t=4),
+            in_=base_weight.rearrange("(t p) i -> p t i", p=P),
+        )
+        for j0, j1 in X_LOADS[1:]:
+            load_x(j0, j1)
+
+        warm = keep.tile([P, 2], F32)
+        nc.vector.memset(warm[:], 0.0)
+        nc.scalar.activation(out=warm[:, 1:2], in_=warm[:, 0:1], func=ACT.Exp)
+        ident = keep.tile([P, P], BF16)
+        make_identity(nc, ident[:])
+        perm = keep.tile([P, P], BF16)
+        perm_v = perm[:].rearrange("p (c q a e) -> p c q a e", c=2, q=4, a=4)
+        ident_v = ident[:].rearrange("p (c a q e) -> p c a q e", c=2, a=4, q=4)
+        for q in range(4):
+            nc.vector.tensor_copy(out=perm_v[:, :, q, :, :], in_=ident_v[:, :, :, q, :])
+        negg = keep.tile([P, GRID], F32)
+        nc.vector.tensor_scalar(out=negg[:], in0=gb[:], scalar1=-1.0, scalar2=None, op0=ALU.mult)
+
+        def permute(dst, src, z0, z1):
+            dst_w = dst[:].bitcast(F32).rearrange("p (z q a w) -> p z q a w", q=4, a=4, w=2)
+            src_w = src[:].bitcast(F32).rearrange("p (z a q w) -> p z a q w", q=4, a=4, w=2)
+            for q in range(4):
+                nc.vector.tensor_copy(out=dst_w[:, z0:z1, q, :, :], in_=src_w[:, z0:z1, :, q, :])
+
+        def transpose4(dst, src):
+            pt = ps_a.tile([P, 4 * P], BF16, tag="a")
+            for r in range(4):
+                nc.tensor.transpose(pt[:, r * P : (r + 1) * P], src[:, r * P : (r + 1) * P], ident[:])
+            nc.vector.tensor_copy(out=dst, in_=pt[:])
+
+        xpm = keep.tile([P, NJ * FEAT], BF16)
+        xT = keep.tile([P, BATCH], BF16)
+
+        def x_group(j0, j1):
+            permute(xpm, xin, 2 * j0, 2 * j1)
+            for j in range(j0, j1, 4):
+                transpose4(xT[:, j * P : (j + 4) * P], xpm[:, j * FEAT : (j + 4) * FEAT])
+
+        x_group(*X_LOADS[0])
+
+        def squares(stage):
+            u, h = divmod(stage, 2)
+            cols = slice(u * CH, (u + 1) * CH)
+            if stage in POOL_STAGES:
+                sq = sqp.tile([P, 4, CH], F32, tag="sqp")
+                for t in range(4):
+                    g = 4 * h + t
+                    nc.gpsimd.tensor_scalar(
+                        out=sq[:, t, :], in0=xT[:, cols], scalar1=1.0, scalar2=negg[:, g : g + 1],
+                        op0=ALU.mult, op1=ALU.add,
+                    )
+                    nc.gpsimd.tensor_tensor(out=sq[:, t, :], in0=sq[:, t, :], in1=sq[:, t, :], op=ALU.mult)
+            else:
+                sq = sqa.tile([P, 4, CH], F32, tag="sqa")
+                for t in range(4):
+                    g = 4 * h + t
+                    nc.scalar.activation(
+                        out=sq[:, t, :], in_=xT[:, cols], func=ACT.Square,
+                        bias=negg[:, g : g + 1], scale=1.0,
+                    )
+            return sq
+
+        bwpm = keep.tile([P, 4 * FEAT], BF16)
+        permute(bwpm, bwin, 0, 8)
+        bwT = keep.tile([P, OUTS], BF16)
+        transpose4(bwT[:], bwpm)
+
+        wgrp = keep.tile([P, 2, OUTS, 4], BF16, align_bytes=64)
+        for h in range(2):
+            for ob in range(4):
+                pw = ps_a.tile([P, 4, P], F32, tag="a")
+                for t in range(4):
+                    nc.tensor.matmul(
+                        out=pw[:, t, :], lhsT=perm[:], rhs=wraw[:, 4 * h + t, ob * P : (ob + 1) * P],
+                        start=True, stop=True,
+                    )
+                nc.vector.tensor_copy(
+                    out=wgrp[:, h, ob * P : (ob + 1) * P, :], in_=pw[:].rearrange("p t o -> p o t")
+                )
+        wcodes = keep.tile([P, 2 * OUTS], U32, align_bytes=64)
+        wscl = keep.tile([P, 2 * OUTS], U8, align_bytes=64)
+        nc.vector.quantize_mx(
+            out=wcodes[:].bitcast(FP8X4), scales=wscl[:], in_=wgrp[:].rearrange("p h o t -> p (h o t)")
+        )
+
+        for j0, j1 in X_LOADS[1:]:
+            x_group(j0, j1)
+
+        out_view = out.rearrange("(p j) o -> p j o", j=NJ)
+        for u in range(N_CH):
+            res = []
+            for m in range(JCH // JRES):
+                rt = rp.tile([P, JRES, OUTS], F32, tag="res")
+                res.append(rt)
+                for r in range(JRES):
+                    j = u * JCH + m * JRES + r
+                    accb = ps_a.tile([P, OUTS], F32, tag="a")
+                    nc.tensor.matmul(
+                        out=accb[:], lhsT=xT[:, j * P : (j + 1) * P], rhs=bwT[:], start=True, stop=True
+                    )
+                    nc.vector.tensor_copy(out=rt[:, r, :], in_=accb[:])
+            codes = []
+            scls = []
+            for h in range(2):
+                sq = squares(2 * u + h)
+                grouped = gp.tile([P, CH, 4], BF16, tag="grouped", align_bytes=64)
+                nc.scalar.activation(
+                    out=grouped[:].rearrange("p (c i) t -> p c t i", i=4),
+                    in_=sq[:].rearrange("p t (c i) -> p c t i", i=4),
+                    func=ACT.Exp,
+                    scale=-20.0,
+                )
+                cd = cp.tile([P, CH], U32, tag="codes", align_bytes=64)
+                sc = cp.tile([P, CH], U8, tag="scl", align_bytes=64)
+                nc.vector.quantize_mx(
+                    out=cd[:].bitcast(FP8X4), scales=sc[:], in_=grouped[:].rearrange("p c t -> p (c t)")
+                )
+                codes.append(cd)
+                scls.append(sc)
+            for m in range(JCH // JRES):
+                rt = res[m]
+                for r in range(JRES):
+                    lo = (m * JRES + r) * P
+                    acc = ps_m.tile([P, OUTS], F32, tag="m")
+                    for h in range(2):
+                        nc.tensor.matmul_mx(
+                            out=acc[:],
+                            lhsT=codes[h][:, lo : lo + P].bitcast(FP8X4),
+                            lhsT_scale=scls[h][:, lo : lo + P],
+                            rhs=wcodes[:, h * OUTS : (h + 1) * OUTS].bitcast(FP8X4),
+                            rhs_scale=wscl[:, h * OUTS : (h + 1) * OUTS],
+                            start=(h == 0),
+                            stop=(h == 1),
+                        )
+                    nc.vector.tensor_tensor(out=rt[:, r, :], in0=acc[:], in1=rt[:, r, :], op=ALU.add)
+                j0 = u * JCH + m * JRES
+                nc.sync.dma_start(out=out_view[:, j0 : j0 + JRES, :], in_=rt[:])

@@ -17,23 +17,35 @@ FEAT = 128
 OUTS = 512
 GRID = 8
 NJ = BATCH // P
-CH = 1024
-JCH = CH // P
-N_CH = BATCH // CH
 JRES = 4
 FLOPS = 2 * BATCH * (FEAT * GRID) * OUTS + 2 * BATCH * FEAT * OUTS
 
-POOL_STAGES = (2, 5, 7, 10, 13, 15)
-X_LOADS = ((0, 8), (8, 24), (24, 64))
+CHUNKS = (2, 2, 4, 8, 8, 8, 8, 8, 8, 4, 2, 2)
+STARTS = tuple(sum(CHUNKS[:c]) for c in range(len(CHUNKS)))
+X_LOADS = ((0, 2), (2, 8), (8, 16), (16, 40), (40, 64))
+POOL_EXTRA = (3, 4, 5, 6, 7)
+VEC_CHUNKS = (4, 5, 6, 7, 8)
+POOL_W = 512
+
+
+def owner(c, h, t):
+    if c == 0:
+        return "scalar"
+    if t == 0:
+        return "gpsimd"
+    if t == 1 and h == 0 and c in POOL_EXTRA:
+        return "gpsimd"
+    if t == 1 and h == 1 and c in VEC_CHUNKS:
+        return "vector"
+    return "scalar"
 
 
 def tile_rbfkanlayer_t_kernel(tc, x, spline_weight, base_weight, grid, out):
     nc = tc.nc
     with ExitStack() as stack:
         keep = stack.enter_context(tc.tile_pool(name="keep", bufs=1))
-        sqa = stack.enter_context(tc.tile_pool(name="sqa", bufs=2))
-        sqp = stack.enter_context(tc.tile_pool(name="sqp", bufs=2))
-        gp = stack.enter_context(tc.tile_pool(name="gp", bufs=2))
+        sqp = stack.enter_context(tc.tile_pool(name="sqp", bufs=4))
+        gp = stack.enter_context(tc.tile_pool(name="gp", bufs=3))
         cp = stack.enter_context(tc.tile_pool(name="cp", bufs=4))
         rp = stack.enter_context(tc.tile_pool(name="rp", bufs=4))
         ps_a = stack.enter_context(tc.psum_pool(name="ps_a", bufs=4))
@@ -47,7 +59,8 @@ def tile_rbfkanlayer_t_kernel(tc, x, spline_weight, base_weight, grid, out):
         def load_x(j0, j1):
             nc.sync.dma_start(out=xin[:, j0 * FEAT : j1 * FEAT], in_=x_view[:, j0 * FEAT : j1 * FEAT])
 
-        load_x(*X_LOADS[0])
+        for j0, j1 in X_LOADS[:3]:
+            load_x(j0, j1)
         wraw = keep.tile([P, GRID, OUTS], BF16)
         nc.sync.dma_start(
             out=wraw[:].rearrange("p g o -> p (g o)"),
@@ -58,7 +71,7 @@ def tile_rbfkanlayer_t_kernel(tc, x, spline_weight, base_weight, grid, out):
             out=bwin[:].rearrange("p (t i) -> p t i", t=4),
             in_=base_weight.rearrange("(t p) i -> p t i", p=P),
         )
-        for j0, j1 in X_LOADS[1:]:
+        for j0, j1 in X_LOADS[3:]:
             load_x(j0, j1)
 
         warm = keep.tile([P, 2], F32)
@@ -66,11 +79,6 @@ def tile_rbfkanlayer_t_kernel(tc, x, spline_weight, base_weight, grid, out):
         nc.scalar.activation(out=warm[:, 1:2], in_=warm[:, 0:1], func=ACT.Exp)
         ident = keep.tile([P, P], BF16)
         make_identity(nc, ident[:])
-        perm = keep.tile([P, P], BF16)
-        perm_v = perm[:].rearrange("p (c q a e) -> p c q a e", c=2, q=4, a=4)
-        ident_v = ident[:].rearrange("p (c a q e) -> p c a q e", c=2, a=4, q=4)
-        for q in range(4):
-            nc.vector.tensor_copy(out=perm_v[:, :, q, :, :], in_=ident_v[:, :, :, q, :])
         negg = keep.tile([P, GRID], F32)
         nc.vector.tensor_scalar(out=negg[:], in0=gb[:], scalar1=-1.0, scalar2=None, op0=ALU.mult)
 
@@ -80,9 +88,9 @@ def tile_rbfkanlayer_t_kernel(tc, x, spline_weight, base_weight, grid, out):
             for q in range(4):
                 nc.vector.tensor_copy(out=dst_w[:, z0:z1, q, :, :], in_=src_w[:, z0:z1, :, q, :])
 
-        def transpose4(dst, src):
-            pt = ps_a.tile([P, 4 * P], BF16, tag="a")
-            for r in range(4):
+        def transposes(dst, src, n):
+            pt = ps_a.tile([P, n * P], BF16, tag="a")
+            for r in range(n):
                 nc.tensor.transpose(pt[:, r * P : (r + 1) * P], src[:, r * P : (r + 1) * P], ident[:])
             nc.vector.tensor_copy(out=dst, in_=pt[:])
 
@@ -92,37 +100,17 @@ def tile_rbfkanlayer_t_kernel(tc, x, spline_weight, base_weight, grid, out):
         def x_group(j0, j1):
             permute(xpm, xin, 2 * j0, 2 * j1)
             for j in range(j0, j1, 4):
-                transpose4(xT[:, j * P : (j + 4) * P], xpm[:, j * FEAT : (j + 4) * FEAT])
+                n = min(4, j1 - j)
+                transposes(xT[:, j * P : (j + n) * P], xpm[:, j * FEAT : (j + n) * FEAT], n)
 
-        x_group(*X_LOADS[0])
+        for j0, j1 in X_LOADS[:3]:
+            x_group(j0, j1)
 
-        def squares(stage):
-            u, h = divmod(stage, 2)
-            cols = slice(u * CH, (u + 1) * CH)
-            if stage in POOL_STAGES:
-                sq = sqp.tile([P, 4, CH], F32, tag="sqp")
-                for t in range(4):
-                    g = 4 * h + t
-                    nc.gpsimd.tensor_scalar(
-                        out=sq[:, t, :], in0=xT[:, cols], scalar1=1.0, scalar2=negg[:, g : g + 1],
-                        op0=ALU.mult, op1=ALU.add,
-                    )
-                    nc.gpsimd.tensor_tensor(out=sq[:, t, :], in0=sq[:, t, :], in1=sq[:, t, :], op=ALU.mult)
-            else:
-                sq = sqa.tile([P, 4, CH], F32, tag="sqa")
-                for t in range(4):
-                    g = 4 * h + t
-                    nc.scalar.activation(
-                        out=sq[:, t, :], in_=xT[:, cols], func=ACT.Square,
-                        bias=negg[:, g : g + 1], scale=1.0,
-                    )
-            return sq
-
-        bwpm = keep.tile([P, 4 * FEAT], BF16)
-        permute(bwpm, bwin, 0, 8)
-        bwT = keep.tile([P, OUTS], BF16)
-        transpose4(bwT[:], bwpm)
-
+        perm = keep.tile([P, P], BF16)
+        perm_v = perm[:].rearrange("p (c q a e) -> p c q a e", c=2, q=4, a=4)
+        ident_v = ident[:].rearrange("p (c a q e) -> p c a q e", c=2, a=4, q=4)
+        for q in range(4):
+            nc.vector.tensor_copy(out=perm_v[:, :, q, :, :], in_=ident_v[:, :, :, q, :])
         wgrp = keep.tile([P, 2, OUTS, 4], BF16, align_bytes=64)
         for h in range(2):
             for ob in range(4):
@@ -140,56 +128,111 @@ def tile_rbfkanlayer_t_kernel(tc, x, spline_weight, base_weight, grid, out):
         nc.vector.quantize_mx(
             out=wcodes[:].bitcast(FP8X4), scales=wscl[:], in_=wgrp[:].rearrange("p h o t -> p (h o t)")
         )
+        bwpm = keep.tile([P, 4 * FEAT], BF16)
+        permute(bwpm, bwin, 0, 8)
+        bwT = keep.tile([P, OUTS], BF16)
+        transposes(bwT[:], bwpm, 4)
 
-        for j0, j1 in X_LOADS[1:]:
+        for j0, j1 in X_LOADS[3:]:
             x_group(j0, j1)
 
-        out_view = out.rearrange("(p j) o -> p j o", j=NJ)
-        for u in range(N_CH):
-            res = []
-            for m in range(JCH // JRES):
-                rt = rp.tile([P, JRES, OUTS], F32, tag="res")
-                res.append(rt)
-                for r in range(JRES):
-                    j = u * JCH + m * JRES + r
+        def squares(s):
+            c, h = divmod(s, 2)
+            w = CHUNKS[c] * P
+            xs = xT[:, STARTS[c] * P : STARTS[c] * P + w]
+            sq = sqp.tile([P, 4, w], F32, tag="sq")
+            for t in range(4):
+                g = 4 * h + t
+                who = owner(c, h, t)
+                if who == "gpsimd":
+                    nc.gpsimd.tensor_scalar(
+                        out=sq[:, t, :], in0=xs, scalar1=1.0, scalar2=negg[:, g : g + 1],
+                        op0=ALU.mult, op1=ALU.add,
+                    )
+                    for k in range(0, w, POOL_W):
+                        part = sq[:, t, k : min(k + POOL_W, w)]
+                        nc.gpsimd.tensor_tensor(out=part, in0=part, in1=part, op=ALU.mult)
+                elif who == "vector":
+                    nc.vector.tensor_scalar(
+                        out=sq[:, t, :], in0=xs, scalar1=negg[:, g : g + 1], scalar2=None, op0=ALU.add
+                    )
+                    nc.vector.tensor_tensor(out=sq[:, t, :], in0=sq[:, t, :], in1=sq[:, t, :], op=ALU.mult)
+                else:
+                    nc.scalar.activation(
+                        out=sq[:, t, :], in_=xs, func=ACT.Square, bias=negg[:, g : g + 1], scale=1.0
+                    )
+            return sq
+
+        def exp_quantise(s, sq):
+            w = CHUNKS[s // 2] * P
+            grouped = gp.tile([P, w, 4], BF16, tag="grouped", align_bytes=64)
+            nc.scalar.activation(
+                out=grouped[:].rearrange("p (c i) t -> p c t i", i=4),
+                in_=sq[:].rearrange("p t (c i) -> p c t i", i=4),
+                func=ACT.Exp,
+                scale=-20.0,
+            )
+            cd = cp.tile([P, w], U32, tag="codes", align_bytes=64)
+            sc = cp.tile([P, w], U8, tag="scl", align_bytes=64)
+            nc.vector.quantize_mx(
+                out=cd[:].bitcast(FP8X4), scales=sc[:], in_=grouped[:].rearrange("p c t -> p (c t)")
+            )
+            return cd, sc
+
+        def base(c):
+            tiles = []
+            for m in range(0, CHUNKS[c], JRES):
+                n = min(JRES, CHUNKS[c] - m)
+                rt = rp.tile([P, n, OUTS], F32, tag="res")
+                tiles.append(rt)
+                for r in range(n):
+                    j = STARTS[c] + m + r
                     accb = ps_a.tile([P, OUTS], F32, tag="a")
                     nc.tensor.matmul(
                         out=accb[:], lhsT=xT[:, j * P : (j + 1) * P], rhs=bwT[:], start=True, stop=True
                     )
                     nc.vector.tensor_copy(out=rt[:, r, :], in_=accb[:])
-            codes = []
-            scls = []
-            for h in range(2):
-                sq = squares(2 * u + h)
-                grouped = gp.tile([P, CH, 4], BF16, tag="grouped", align_bytes=64)
-                nc.scalar.activation(
-                    out=grouped[:].rearrange("p (c i) t -> p c t i", i=4),
-                    in_=sq[:].rearrange("p t (c i) -> p c t i", i=4),
-                    func=ACT.Exp,
-                    scale=-20.0,
-                )
-                cd = cp.tile([P, CH], U32, tag="codes", align_bytes=64)
-                sc = cp.tile([P, CH], U8, tag="scl", align_bytes=64)
-                nc.vector.quantize_mx(
-                    out=cd[:].bitcast(FP8X4), scales=sc[:], in_=grouped[:].rearrange("p c t -> p (c t)")
-                )
-                codes.append(cd)
-                scls.append(sc)
-            for m in range(JCH // JRES):
-                rt = res[m]
-                for r in range(JRES):
-                    lo = (m * JRES + r) * P
+            return tiles
+
+        out_view = out.rearrange("(p j) o -> p j o", j=NJ)
+
+        def spline(c, tiles, quantised):
+            last = c == len(CHUNKS) - 1
+            for m in range(0, CHUNKS[c], JRES):
+                n = min(JRES, CHUNKS[c] - m)
+                rt = tiles[m // JRES]
+                for r in range(n):
+                    lo = (m + r) * P
                     acc = ps_m.tile([P, OUTS], F32, tag="m")
                     for h in range(2):
+                        cd, sc = quantised[h]
                         nc.tensor.matmul_mx(
                             out=acc[:],
-                            lhsT=codes[h][:, lo : lo + P].bitcast(FP8X4),
-                            lhsT_scale=scls[h][:, lo : lo + P],
+                            lhsT=cd[:, lo : lo + P].bitcast(FP8X4),
+                            lhsT_scale=sc[:, lo : lo + P],
                             rhs=wcodes[:, h * OUTS : (h + 1) * OUTS].bitcast(FP8X4),
                             rhs_scale=wscl[:, h * OUTS : (h + 1) * OUTS],
                             start=(h == 0),
                             stop=(h == 1),
                         )
                     nc.vector.tensor_tensor(out=rt[:, r, :], in0=acc[:], in1=rt[:, r, :], op=ALU.add)
-                j0 = u * JCH + m * JRES
-                nc.sync.dma_start(out=out_view[:, j0 : j0 + JRES, :], in_=rt[:])
+                    if last:
+                        j = STARTS[c] + m + r
+                        nc.sync.dma_start(out=out_view[:, j : j + 1, :], in_=rt[:, r : r + 1, :])
+                if not last:
+                    j = STARTS[c] + m
+                    nc.sync.dma_start(out=out_view[:, j : j + n, :], in_=rt[:])
+
+        n_stages = 2 * len(CHUNKS)
+        results = {0: base(0)}
+        sq_tiles = {0: squares(0)}
+        quantised = {}
+        for s in range(n_stages):
+            c, h = divmod(s, 2)
+            if h == 0 and c + 1 < len(CHUNKS):
+                results[c + 1] = base(c + 1)
+            if s + 1 < n_stages:
+                sq_tiles[s + 1] = squares(s + 1)
+            quantised[s] = exp_quantise(s, sq_tiles[s])
+            if h == 1:
+                spline(c, results[c], (quantised[s - 1], quantised[s]))

@@ -23,21 +23,7 @@ FLOPS = 2 * BATCH * (FEAT * GRID) * OUTS + 2 * BATCH * FEAT * OUTS
 CHUNKS = (2, 2, 4, 8, 8, 8, 8, 8, 8, 4, 2, 2)
 STARTS = tuple(sum(CHUNKS[:c]) for c in range(len(CHUNKS)))
 X_LOADS = ((0, 2), (2, 8), (8, 16), (16, 40), (40, 64))
-POOL_EXTRA = (3, 4, 5, 6, 7)
-VEC_CHUNKS = (4, 5, 6, 7, 8)
-POOL_W = 512
-
-
-def owner(c, h, t):
-    if c == 0:
-        return "scalar"
-    if t == 0:
-        return "gpsimd"
-    if t == 1 and h == 0 and c in POOL_EXTRA:
-        return "gpsimd"
-    if t == 1 and h == 1 and c in VEC_CHUNKS:
-        return "vector"
-    return "scalar"
+POOL_COLS = {8: 1536, 4: 512}
 
 
 def tile_rbfkanlayer_t_kernel(tc, x, spline_weight, base_weight, grid, out):
@@ -45,7 +31,7 @@ def tile_rbfkanlayer_t_kernel(tc, x, spline_weight, base_weight, grid, out):
     with ExitStack() as stack:
         keep = stack.enter_context(tc.tile_pool(name="keep", bufs=1))
         sqp = stack.enter_context(tc.tile_pool(name="sqp", bufs=4))
-        gp = stack.enter_context(tc.tile_pool(name="gp", bufs=3))
+        gp = stack.enter_context(tc.tile_pool(name="gp", bufs=4))
         cp = stack.enter_context(tc.tile_pool(name="cp", bufs=4))
         rp = stack.enter_context(tc.tile_pool(name="rp", bufs=4))
         ps_a = stack.enter_context(tc.psum_pool(name="ps_a", bufs=4))
@@ -136,32 +122,38 @@ def tile_rbfkanlayer_t_kernel(tc, x, spline_weight, base_weight, grid, out):
         for j0, j1 in X_LOADS[3:]:
             x_group(j0, j1)
 
-        def squares(s):
-            c, h = divmod(s, 2)
+        def stage_view(s):
+            c = s // 2
             w = CHUNKS[c] * P
-            xs = xT[:, STARTS[c] * P : STARTS[c] * P + w]
+            return w, xT[:, STARTS[c] * P : STARTS[c] * P + w]
+
+        def pool_squares(s, neg_grid):
+            w, xs = stage_view(s)
             sq = sqp.tile([P, 4, w], F32, tag="sq")
+            left = POOL_COLS.get(CHUNKS[s // 2], 0)
             for t in range(4):
-                g = 4 * h + t
-                who = owner(c, h, t)
-                if who == "gpsimd":
+                k = min(left, w)
+                left -= k
+                if k > 0:
+                    g = 4 * (s % 2) + t
                     nc.gpsimd.tensor_scalar(
-                        out=sq[:, t, :], in0=xs, scalar1=1.0, scalar2=negg[:, g : g + 1],
+                        out=sq[:, t, 0:k], in0=xs[:, 0:k], scalar1=1.0, scalar2=neg_grid[:, g : g + 1],
                         op0=ALU.mult, op1=ALU.add,
                     )
-                    for k in range(0, w, POOL_W):
-                        part = sq[:, t, k : min(k + POOL_W, w)]
-                        nc.gpsimd.tensor_tensor(out=part, in0=part, in1=part, op=ALU.mult)
-                elif who == "vector":
-                    nc.vector.tensor_scalar(
-                        out=sq[:, t, :], in0=xs, scalar1=negg[:, g : g + 1], scalar2=None, op0=ALU.add
-                    )
-                    nc.vector.tensor_tensor(out=sq[:, t, :], in0=sq[:, t, :], in1=sq[:, t, :], op=ALU.mult)
-                else:
-                    nc.scalar.activation(
-                        out=sq[:, t, :], in_=xs, func=ACT.Square, bias=negg[:, g : g + 1], scale=1.0
-                    )
+                    nc.gpsimd.tensor_tensor(out=sq[:, t, 0:k], in0=sq[:, t, 0:k], in1=sq[:, t, 0:k], op=ALU.mult)
             return sq
+
+        def scalar_squares(s, sq):
+            w, xs = stage_view(s)
+            left = POOL_COLS.get(CHUNKS[s // 2], 0)
+            for t in range(4):
+                k = min(left, w)
+                left -= k
+                if k < w:
+                    g = 4 * (s % 2) + t
+                    nc.scalar.activation(
+                        out=sq[:, t, k:w], in_=xs[:, k:w], func=ACT.Square, bias=negg[:, g : g + 1], scale=1.0
+                    )
 
         def exp_quantise(s, sq):
             w = CHUNKS[s // 2] * P
@@ -177,7 +169,10 @@ def tile_rbfkanlayer_t_kernel(tc, x, spline_weight, base_weight, grid, out):
             nc.vector.quantize_mx(
                 out=cd[:].bitcast(FP8X4), scales=sc[:], in_=grouped[:].rearrange("p c t -> p (c t)")
             )
-            return cd, sc
+            return cd, sc, grouped
+
+        def gate(grouped):
+            return negg
 
         def base(c):
             tiles = []
@@ -205,7 +200,7 @@ def tile_rbfkanlayer_t_kernel(tc, x, spline_weight, base_weight, grid, out):
                     lo = (m + r) * P
                     acc = ps_m.tile([P, OUTS], F32, tag="m")
                     for h in range(2):
-                        cd, sc = quantised[h]
+                        cd, sc = quantised[h][0:2]
                         nc.tensor.matmul_mx(
                             out=acc[:],
                             lhsT=cd[:, lo : lo + P].bitcast(FP8X4),
@@ -225,14 +220,20 @@ def tile_rbfkanlayer_t_kernel(tc, x, spline_weight, base_weight, grid, out):
 
         n_stages = 2 * len(CHUNKS)
         results = {0: base(0)}
-        sq_tiles = {0: squares(0)}
+        sq_tiles = {0: pool_squares(0, negg), 1: pool_squares(1, negg)}
+        scalar_squares(0, sq_tiles[0])
         quantised = {}
         for s in range(n_stages):
             c, h = divmod(s, 2)
             if h == 0 and c + 1 < len(CHUNKS):
                 results[c + 1] = base(c + 1)
             if s + 1 < n_stages:
-                sq_tiles[s + 1] = squares(s + 1)
+                scalar_squares(s + 1, sq_tiles[s + 1])
             quantised[s] = exp_quantise(s, sq_tiles[s])
+            if s + 2 < n_stages:
+                if POOL_COLS.get(CHUNKS[(s + 2) // 2], 0) > 0:
+                    sq_tiles[s + 2] = pool_squares(s + 2, gate(quantised[s][2]))
+                else:
+                    sq_tiles[s + 2] = pool_squares(s + 2, negg)
             if h == 1:
                 spline(c, results[c], (quantised[s - 1], quantised[s]))

@@ -20,10 +20,33 @@ NJ = BATCH // P
 JRES = 4
 FLOPS = 2 * BATCH * (FEAT * GRID) * OUTS + 2 * BATCH * FEAT * OUTS
 
-CHUNKS = (2, 2, 4, 8, 8, 8, 8, 8, 8, 4, 2, 2)
+CHUNKS = (8, 8, 8, 8, 8, 8, 8, 8)
 STARTS = tuple(sum(CHUNKS[:c]) for c in range(len(CHUNKS)))
-X_LOADS = ((0, 2), (2, 8), (8, 16), (16, 40), (40, 64))
-POOL_COLS = {8: 1536, 4: 512}
+X_LOADS = ((0, 8), (8, 24), (24, 64))
+POOL_EXTRA = (1, 2, 4, 5, 7)
+VEC_CHUNKS = (1, 2, 3, 4, 5, 6, 7)
+BLOCKS = {7: (4, 2, 2)}
+STORE = {(7, 6): 1}
+POOL_W = 512
+
+
+def owner(c, h, t):
+    if c == 0:
+        return "scalar"
+    if t == 0:
+        return "gpsimd"
+    if t == 1 and h == 0 and c in POOL_EXTRA:
+        return "gpsimd"
+    if t == 1 and h == 1 and c in VEC_CHUNKS:
+        return "vector"
+    return "scalar"
+    if t == 0:
+        return "gpsimd"
+    if t == 1 and h == 0 and c in POOL_EXTRA:
+        return "gpsimd"
+    if t == 1 and h == 1 and c in VEC_CHUNKS:
+        return "vector"
+    return "scalar"
 
 
 def tile_rbfkanlayer_t_kernel(tc, x, spline_weight, base_weight, grid, out):
@@ -31,7 +54,7 @@ def tile_rbfkanlayer_t_kernel(tc, x, spline_weight, base_weight, grid, out):
     with ExitStack() as stack:
         keep = stack.enter_context(tc.tile_pool(name="keep", bufs=1))
         sqp = stack.enter_context(tc.tile_pool(name="sqp", bufs=4))
-        gp = stack.enter_context(tc.tile_pool(name="gp", bufs=4))
+        gp = stack.enter_context(tc.tile_pool(name="gp", bufs=3))
         cp = stack.enter_context(tc.tile_pool(name="cp", bufs=4))
         rp = stack.enter_context(tc.tile_pool(name="rp", bufs=4))
         ps_a = stack.enter_context(tc.psum_pool(name="ps_a", bufs=4))
@@ -45,7 +68,7 @@ def tile_rbfkanlayer_t_kernel(tc, x, spline_weight, base_weight, grid, out):
         def load_x(j0, j1):
             nc.sync.dma_start(out=xin[:, j0 * FEAT : j1 * FEAT], in_=x_view[:, j0 * FEAT : j1 * FEAT])
 
-        for j0, j1 in X_LOADS[:3]:
+        for j0, j1 in X_LOADS[:1]:
             load_x(j0, j1)
         wraw = keep.tile([P, GRID, OUTS], BF16)
         nc.sync.dma_start(
@@ -57,7 +80,7 @@ def tile_rbfkanlayer_t_kernel(tc, x, spline_weight, base_weight, grid, out):
             out=bwin[:].rearrange("p (t i) -> p t i", t=4),
             in_=base_weight.rearrange("(t p) i -> p t i", p=P),
         )
-        for j0, j1 in X_LOADS[3:]:
+        for j0, j1 in X_LOADS[1:]:
             load_x(j0, j1)
 
         warm = keep.tile([P, 2], F32)
@@ -89,7 +112,7 @@ def tile_rbfkanlayer_t_kernel(tc, x, spline_weight, base_weight, grid, out):
                 n = min(4, j1 - j)
                 transposes(xT[:, j * P : (j + n) * P], xpm[:, j * FEAT : (j + n) * FEAT], n)
 
-        for j0, j1 in X_LOADS[:3]:
+        for j0, j1 in X_LOADS[:1]:
             x_group(j0, j1)
 
         perm = keep.tile([P, P], BF16)
@@ -119,48 +142,41 @@ def tile_rbfkanlayer_t_kernel(tc, x, spline_weight, base_weight, grid, out):
         bwT = keep.tile([P, OUTS], BF16)
         transposes(bwT[:], bwpm, 4)
 
-        for j0, j1 in X_LOADS[3:]:
+        for j0, j1 in X_LOADS[1:]:
             x_group(j0, j1)
 
-        def stage_view(s):
-            c = s // 2
+        def squares(s):
+            c, h = divmod(s, 2)
             w = CHUNKS[c] * P
-            return w, xT[:, STARTS[c] * P : STARTS[c] * P + w]
-
-        def pool_squares(s, neg_grid):
-            w, xs = stage_view(s)
+            xs = xT[:, STARTS[c] * P : STARTS[c] * P + w]
             sq = sqp.tile([P, 4, w], F32, tag="sq")
-            left = POOL_COLS.get(CHUNKS[s // 2], 0)
             for t in range(4):
-                k = min(left, w)
-                left -= k
-                if k > 0:
-                    g = 4 * (s % 2) + t
+                g = 4 * h + t
+                who = owner(c, h, t)
+                if who == "gpsimd":
                     nc.gpsimd.tensor_scalar(
-                        out=sq[:, t, 0:k], in0=xs[:, 0:k], scalar1=1.0, scalar2=neg_grid[:, g : g + 1],
+                        out=sq[:, t, :], in0=xs, scalar1=1.0, scalar2=negg[:, g : g + 1],
                         op0=ALU.mult, op1=ALU.add,
                     )
-                    nc.gpsimd.tensor_tensor(out=sq[:, t, 0:k], in0=sq[:, t, 0:k], in1=sq[:, t, 0:k], op=ALU.mult)
+                    for k in range(0, w, POOL_W):
+                        part = sq[:, t, k : min(k + POOL_W, w)]
+                        nc.gpsimd.tensor_tensor(out=part, in0=part, in1=part, op=ALU.mult)
+                elif who == "vector":
+                    nc.vector.tensor_scalar(
+                        out=sq[:, t, :], in0=xs, scalar1=negg[:, g : g + 1], scalar2=None, op0=ALU.add
+                    )
+                    nc.vector.tensor_tensor(out=sq[:, t, :], in0=sq[:, t, :], in1=sq[:, t, :], op=ALU.mult)
+                else:
+                    nc.scalar.activation(
+                        out=sq[:, t, :], in_=xs, func=ACT.Square, bias=negg[:, g : g + 1], scale=1.0
+                    )
             return sq
 
-        def scalar_squares(s, sq):
-            w, xs = stage_view(s)
-            left = POOL_COLS.get(CHUNKS[s // 2], 0)
-            for t in range(4):
-                k = min(left, w)
-                left -= k
-                if k < w:
-                    g = 4 * (s % 2) + t
-                    nc.scalar.activation(
-                        out=sq[:, t, k:w], in_=xs[:, k:w], func=ACT.Square, bias=negg[:, g : g + 1], scale=1.0
-                    )
-
-        def exp_quantise(s, sq):
-            w = CHUNKS[s // 2] * P
+        def exp_quantise(sq, k0, w):
             grouped = gp.tile([P, w, 4], BF16, tag="grouped", align_bytes=64)
             nc.scalar.activation(
                 out=grouped[:].rearrange("p (c i) t -> p c t i", i=4),
-                in_=sq[:].rearrange("p t (c i) -> p c t i", i=4),
+                in_=sq[:, :, k0 : k0 + w].rearrange("p t (c i) -> p c t i", i=4),
                 func=ACT.Exp,
                 scale=-20.0,
             )
@@ -169,10 +185,7 @@ def tile_rbfkanlayer_t_kernel(tc, x, spline_weight, base_weight, grid, out):
             nc.vector.quantize_mx(
                 out=cd[:].bitcast(FP8X4), scales=sc[:], in_=grouped[:].rearrange("p c t -> p (c t)")
             )
-            return cd, sc, grouped
-
-        def gate(grouped):
-            return negg
+            return cd, sc
 
         def base(c):
             tiles = []
@@ -191,49 +204,41 @@ def tile_rbfkanlayer_t_kernel(tc, x, spline_weight, base_weight, grid, out):
 
         out_view = out.rearrange("(p j) o -> p j o", j=NJ)
 
-        def spline(c, tiles, quantised):
-            last = c == len(CHUNKS) - 1
-            for m in range(0, CHUNKS[c], JRES):
-                n = min(JRES, CHUNKS[c] - m)
+        def spline(c, tiles, quantised, m0, nj):
+            for m in range(m0, m0 + nj):
                 rt = tiles[m // JRES]
-                for r in range(n):
-                    lo = (m + r) * P
-                    acc = ps_m.tile([P, OUTS], F32, tag="m")
-                    for h in range(2):
-                        cd, sc = quantised[h][0:2]
-                        nc.tensor.matmul_mx(
-                            out=acc[:],
-                            lhsT=cd[:, lo : lo + P].bitcast(FP8X4),
-                            lhsT_scale=sc[:, lo : lo + P],
-                            rhs=wcodes[:, h * OUTS : (h + 1) * OUTS].bitcast(FP8X4),
-                            rhs_scale=wscl[:, h * OUTS : (h + 1) * OUTS],
-                            start=(h == 0),
-                            stop=(h == 1),
-                        )
-                    nc.vector.tensor_tensor(out=rt[:, r, :], in0=acc[:], in1=rt[:, r, :], op=ALU.add)
-                    if last:
-                        j = STARTS[c] + m + r
-                        nc.sync.dma_start(out=out_view[:, j : j + 1, :], in_=rt[:, r : r + 1, :])
-                if not last:
-                    j = STARTS[c] + m
-                    nc.sync.dma_start(out=out_view[:, j : j + n, :], in_=rt[:])
+                r = m % JRES
+                lo = (m - m0) * P
+                acc = ps_m.tile([P, OUTS], F32, tag="m")
+                for h in range(2):
+                    cd, sc = quantised[h]
+                    nc.tensor.matmul_mx(
+                        out=acc[:],
+                        lhsT=cd[:, lo : lo + P].bitcast(FP8X4),
+                        lhsT_scale=sc[:, lo : lo + P],
+                        rhs=wcodes[:, h * OUTS : (h + 1) * OUTS].bitcast(FP8X4),
+                        rhs_scale=wscl[:, h * OUTS : (h + 1) * OUTS],
+                        start=(h == 0),
+                        stop=(h == 1),
+                    )
+                nc.vector.tensor_tensor(out=rt[:, r, :], in0=acc[:], in1=rt[:, r, :], op=ALU.add)
+                n = min(nj, STORE.get((c, m0), JRES))
+                if (m - m0) % n == n - 1:
+                    j = STARTS[c] + m - n + 1
+                    nc.sync.dma_start(out=out_view[:, j : j + n, :], in_=rt[:, r - n + 1 : r + 1, :])
 
-        n_stages = 2 * len(CHUNKS)
+        n_chunks = len(CHUNKS)
         results = {0: base(0)}
-        sq_tiles = {0: pool_squares(0, negg), 1: pool_squares(1, negg)}
-        scalar_squares(0, sq_tiles[0])
-        quantised = {}
-        for s in range(n_stages):
-            c, h = divmod(s, 2)
-            if h == 0 and c + 1 < len(CHUNKS):
+        sq_tiles = {0: squares(0)}
+        for c in range(n_chunks):
+            if c + 1 < n_chunks:
                 results[c + 1] = base(c + 1)
-            if s + 1 < n_stages:
-                scalar_squares(s + 1, sq_tiles[s + 1])
-            quantised[s] = exp_quantise(s, sq_tiles[s])
-            if s + 2 < n_stages:
-                if POOL_COLS.get(CHUNKS[(s + 2) // 2], 0) > 0:
-                    sq_tiles[s + 2] = pool_squares(s + 2, gate(quantised[s][2]))
-                else:
-                    sq_tiles[s + 2] = pool_squares(s + 2, negg)
-            if h == 1:
-                spline(c, results[c], (quantised[s - 1], quantised[s]))
+            sq_tiles[2 * c + 1] = squares(2 * c + 1)
+            m0 = 0
+            for nj in BLOCKS.get(c, (CHUNKS[c],)):
+                first = exp_quantise(sq_tiles[2 * c], m0 * P, nj * P)
+                if m0 == 0 and c + 1 < n_chunks:
+                    sq_tiles[2 * c + 2] = squares(2 * c + 2)
+                second = exp_quantise(sq_tiles[2 * c + 1], m0 * P, nj * P)
+                spline(c, results[c], (first, second), m0, nj)
+                m0 += nj

@@ -18,33 +18,20 @@ OUTS = 512
 GRID = 8
 NJ = BATCH // P
 JRES = 4
+UNITS = (4, 8, 8, 8, 8, 8, 8, 4, 4, 4)
+NU = len(UNITS)
+FIRST = tuple(sum(UNITS[:u]) for u in range(NU))
 FLOPS = 2 * BATCH * (FEAT * GRID) * OUTS + 2 * BATCH * FEAT * OUTS
 
-CHUNKS = (8, 8, 8, 8, 8, 8, 8, 8)
-STARTS = tuple(sum(CHUNKS[:c]) for c in range(len(CHUNKS)))
-X_LOADS = ((0, 8), (8, 24), (24, 64))
-POOL_EXTRA = (1, 2, 4, 5, 7)
-VEC_CHUNKS = (1, 2, 3, 4, 5, 6, 7)
-BLOCKS = {7: (4, 2, 2)}
-STORE = {(7, 6): 1}
+X_LOADS = ((0, 4), (4, 16), (16, 64))
 POOL_W = 512
+END_BLOCKS = ((0, 2), (2, 4))
 
 
-def owner(c, h, t):
-    if c == 0:
-        return "scalar"
-    if t == 0:
+def owner(u, h, t):
+    if t < (h if u == 0 else 2 if h == 0 and u % 2 else 1):
         return "gpsimd"
-    if t == 1 and h == 0 and c in POOL_EXTRA:
-        return "gpsimd"
-    if t == 1 and h == 1 and c in VEC_CHUNKS:
-        return "vector"
-    return "scalar"
-    if t == 0:
-        return "gpsimd"
-    if t == 1 and h == 0 and c in POOL_EXTRA:
-        return "gpsimd"
-    if t == 1 and h == 1 and c in VEC_CHUNKS:
+    if t == 3 and h == 1 and u % 2 == 0:
         return "vector"
     return "scalar"
 
@@ -52,11 +39,13 @@ def owner(c, h, t):
 def tile_rbfkanlayer_t_kernel(tc, x, spline_weight, base_weight, grid, out):
     nc = tc.nc
     with ExitStack() as stack:
+        stack.enter_context(tc.manual_schedule())
         keep = stack.enter_context(tc.tile_pool(name="keep", bufs=1))
         sqp = stack.enter_context(tc.tile_pool(name="sqp", bufs=4))
+        gates = stack.enter_context(tc.tile_pool(name="gates", bufs=2))
         gp = stack.enter_context(tc.tile_pool(name="gp", bufs=3))
         cp = stack.enter_context(tc.tile_pool(name="cp", bufs=4))
-        rp = stack.enter_context(tc.tile_pool(name="rp", bufs=4))
+        rp = stack.enter_context(tc.tile_pool(name="rp", bufs=6))
         ps_a = stack.enter_context(tc.psum_pool(name="ps_a", bufs=4))
         ps_m = stack.enter_context(tc.psum_pool(name="ps_m", bufs=4))
 
@@ -68,20 +57,22 @@ def tile_rbfkanlayer_t_kernel(tc, x, spline_weight, base_weight, grid, out):
         def load_x(j0, j1):
             nc.sync.dma_start(out=xin[:, j0 * FEAT : j1 * FEAT], in_=x_view[:, j0 * FEAT : j1 * FEAT])
 
-        for j0, j1 in X_LOADS[:1]:
-            load_x(j0, j1)
+        load_x(*X_LOADS[0])
+        load_x(*X_LOADS[1])
         wraw = keep.tile([P, GRID, OUTS], BF16)
-        nc.sync.dma_start(
-            out=wraw[:].rearrange("p g o -> p (g o)"),
-            in_=spline_weight.rearrange("(i g) o -> i (g o)", g=GRID),
-        )
+        w_view = spline_weight.rearrange("(n q e g) o -> q e n (g o)", n=8, q=4, e=4)
+        for q in range(4):
+            for e in range(4):
+                p0 = 32 * q + e
+                nc.sync.dma_start(
+                    out=wraw[p0 : p0 + 29 : 4, :, :].rearrange("p g o -> p (g o)"), in_=w_view[q, e, :, :]
+                )
         bwin = keep.tile([P, 4 * FEAT], BF16)
         nc.sync.dma_start(
             out=bwin[:].rearrange("p (t i) -> p t i", t=4),
             in_=base_weight.rearrange("(t p) i -> p t i", p=P),
         )
-        for j0, j1 in X_LOADS[1:]:
-            load_x(j0, j1)
+        load_x(*X_LOADS[2])
 
         warm = keep.tile([P, 2], F32)
         nc.vector.memset(warm[:], 0.0)
@@ -92,153 +83,198 @@ def tile_rbfkanlayer_t_kernel(tc, x, spline_weight, base_weight, grid, out):
         nc.vector.tensor_scalar(out=negg[:], in0=gb[:], scalar1=-1.0, scalar2=None, op0=ALU.mult)
 
         def permute(dst, src, z0, z1):
-            dst_w = dst[:].bitcast(F32).rearrange("p (z q a w) -> p z q a w", q=4, a=4, w=2)
-            src_w = src[:].bitcast(F32).rearrange("p (z a q w) -> p z a q w", q=4, a=4, w=2)
+            dst_w = dst[:].bitcast(F32).rearrange("p (z q n w) -> p z q n w", q=4, n=8, w=2)
+            src_w = src[:].bitcast(F32).rearrange("p (z n q w) -> p z n q w", q=4, n=8, w=2)
             for q in range(4):
                 nc.vector.tensor_copy(out=dst_w[:, z0:z1, q, :, :], in_=src_w[:, z0:z1, :, q, :])
 
-        def transposes(dst, src, n):
-            pt = ps_a.tile([P, n * P], BF16, tag="a")
-            for r in range(n):
+        def transposes(dst, src):
+            pt = ps_a.tile([P, 4 * P], BF16, tag="a")
+            for r in range(4):
                 nc.tensor.transpose(pt[:, r * P : (r + 1) * P], src[:, r * P : (r + 1) * P], ident[:])
             nc.vector.tensor_copy(out=dst, in_=pt[:])
 
         xpm = keep.tile([P, NJ * FEAT], BF16)
         xT = keep.tile([P, BATCH], BF16)
 
-        def x_group(j0, j1):
-            permute(xpm, xin, 2 * j0, 2 * j1)
-            for j in range(j0, j1, 4):
-                n = min(4, j1 - j)
-                transposes(xT[:, j * P : (j + n) * P], xpm[:, j * FEAT : (j + n) * FEAT], n)
+        def permute_x(j0, j1):
+            permute(xpm, xin, j0, j1)
 
-        for j0, j1 in X_LOADS[:1]:
-            x_group(j0, j1)
+        def transpose_x(q):
+            transposes(xT[:, 4 * q * P : 4 * (q + 1) * P], xpm[:, 4 * q * P : 4 * (q + 1) * P])
 
-        perm = keep.tile([P, P], BF16)
-        perm_v = perm[:].rearrange("p (c q a e) -> p c q a e", c=2, q=4, a=4)
-        ident_v = ident[:].rearrange("p (c a q e) -> p c a q e", c=2, a=4, q=4)
-        for q in range(4):
-            nc.vector.tensor_copy(out=perm_v[:, :, q, :, :], in_=ident_v[:, :, :, q, :])
+        sq_tiles, codes, results, gate = {}, {}, {}, {}
+
+        def width(u):
+            return UNITS[u] * P
+
+        def x_of(u):
+            return xT[:, FIRST[u] * P : FIRST[u] * P + width(u)]
+
+        def transpose_unit(u):
+            for q in range(FIRST[u] // 4, (FIRST[u] + UNITS[u]) // 4):
+                transpose_x(q)
+
+        def squares_gpsimd(u, h):
+            sq_tiles[u, h] = sqp.tile([P, 4, width(u)], F32, tag="sq", name="sq")
+            for t in range(4):
+                if owner(u, h, t) != "gpsimd":
+                    continue
+                g = 4 * h + t
+                plane = sq_tiles[u, h][:, t, :]
+                for k in range(0, width(u), POOL_W):
+                    part = plane[:, k : k + POOL_W]
+                    nc.gpsimd.tensor_scalar(
+                        out=part, in0=x_of(u)[:, k : k + POOL_W], scalar1=1.0,
+                        scalar2=gate.get(u, negg)[:, g : g + 1], op0=ALU.mult, op1=ALU.add,
+                    )
+                    nc.gpsimd.tensor_tensor(out=part, in0=part, in1=part, op=ALU.mult)
+
+        def squares_scalar(u, h):
+            for t in range(4):
+                if owner(u, h, t) == "scalar":
+                    g = 4 * h + t
+                    nc.scalar.activation(
+                        out=sq_tiles[u, h][:, t, :], in_=x_of(u), func=ACT.Square, bias=negg[:, g : g + 1], scale=1.0
+                    )
+
+        def vector_planes(u):
+            return [(h, t) for h in range(2) for t in range(4) if owner(u, h, t) == "vector"]
+
+        def differences_vector(u):
+            for h, t in vector_planes(u):
+                g = 4 * h + t
+                nc.vector.tensor_scalar(
+                    out=sq_tiles[u, h][:, t, :], in0=x_of(u), scalar1=negg[:, g : g + 1], scalar2=None, op0=ALU.add
+                )
+
+        def squares_vector(u):
+            for h, t in vector_planes(u):
+                plane = sq_tiles[u, h][:, t, :]
+                nc.vector.tensor_tensor(out=plane, in0=plane, in1=plane, op=ALU.mult)
+
+        def new_group(u):
+            return gp.tile([P, width(u), 4], BF16, tag="grouped", name="grouped", align_bytes=64)
+
+        def exponential(u, h, grouped, c0, c1):
+            nc.scalar.activation(
+                out=grouped[:, c0:c1, :].rearrange("p (c i) t -> p c t i", i=4),
+                in_=sq_tiles[u, h][:, :, c0:c1].rearrange("p t (c i) -> p c t i", i=4),
+                func=ACT.Exp,
+                scale=-20.0,
+            )
+
+        def new_codes(u):
+            cd = cp.tile([P, width(u)], U32, tag="codes", align_bytes=64)
+            sc = cp.tile([P, width(u)], U8, tag="scl", align_bytes=64)
+            return cd, sc
+
+        def quantise(u, h, grouped, c0, c1):
+            cd, sc = codes[u][h]
+            nc.vector.quantize_mx(
+                out=cd[:, c0:c1].bitcast(FP8X4), scales=sc[:, c0:c1],
+                in_=grouped[:, c0:c1, :].rearrange("p c t -> p (c t)"),
+            )
+
+        def base(u, r):
+            if r % JRES == 0:
+                results[u, r // JRES] = rp.tile([P, JRES, OUTS], F32, tag="res", name="res")
+            j = FIRST[u] + r
+            accb = ps_a.tile([P, OUTS], F32, tag="a")
+            nc.tensor.matmul(out=accb[:], lhsT=xT[:, j * P : (j + 1) * P], rhs=bwT[:], start=True, stop=True)
+            nc.vector.tensor_copy(out=results[u, r // JRES][:, r % JRES, :], in_=accb[:])
+
+        out_view = out.rearrange("(p j) o -> p j o", j=NJ)
+
+        def spline(u, r):
+            rt = results[u, r // JRES]
+            acc = ps_m.tile([P, OUTS], F32, tag="m")
+            for h, (cd, sc) in enumerate(codes[u]):
+                nc.tensor.matmul_mx(
+                    out=acc[:],
+                    lhsT=cd[:, r * P : (r + 1) * P].bitcast(FP8X4),
+                    lhsT_scale=sc[:, r * P : (r + 1) * P],
+                    rhs=wcodes[:, h * OUTS : (h + 1) * OUTS].bitcast(FP8X4),
+                    rhs_scale=wscl[:, h * OUTS : (h + 1) * OUTS],
+                    start=(h == 0),
+                    stop=(h == 1),
+                )
+            nc.vector.tensor_tensor(out=rt[:, r % JRES, :], in0=acc[:], in1=rt[:, r % JRES, :], op=ALU.add)
+
+        def store(u, r0, r1):
+            j = FIRST[u]
+            nc.sync.dma_start(
+                out=out_view[:, j + r0 : j + r1, :], in_=results[u, r0 // JRES][:, r0 % JRES : r0 % JRES + r1 - r0, :]
+            )
+
+        permute_x(*X_LOADS[0])
+        transpose_unit(0)
+        permute_x(*X_LOADS[1])
+        transpose_unit(1)
+        for h in range(2):
+            squares_gpsimd(0, h)
+        differences_vector(0)
+        squares_vector(0)
+        for h in range(2):
+            squares_gpsimd(1, h)
+
         wgrp = keep.tile([P, 2, OUTS, 4], BF16, align_bytes=64)
         for h in range(2):
-            for ob in range(4):
-                pw = ps_a.tile([P, 4, P], F32, tag="a")
-                for t in range(4):
-                    nc.tensor.matmul(
-                        out=pw[:, t, :], lhsT=perm[:], rhs=wraw[:, 4 * h + t, ob * P : (ob + 1) * P],
-                        start=True, stop=True,
-                    )
-                nc.vector.tensor_copy(
-                    out=wgrp[:, h, ob * P : (ob + 1) * P, :], in_=pw[:].rearrange("p t o -> p o t")
-                )
+            nc.vector.tensor_copy(
+                out=wgrp[:, h, :, :].rearrange("p (c i) t -> p c t i", i=4),
+                in_=wraw[:, 4 * h : 4 * h + 4, :].rearrange("p t (c i) -> p c t i", i=4),
+            )
         wcodes = keep.tile([P, 2 * OUTS], U32, align_bytes=64)
         wscl = keep.tile([P, 2 * OUTS], U8, align_bytes=64)
         nc.vector.quantize_mx(
             out=wcodes[:].bitcast(FP8X4), scales=wscl[:], in_=wgrp[:].rearrange("p h o t -> p (h o t)")
         )
         bwpm = keep.tile([P, 4 * FEAT], BF16)
-        permute(bwpm, bwin, 0, 8)
+        permute(bwpm, bwin, 0, 4)
         bwT = keep.tile([P, OUTS], BF16)
-        transposes(bwT[:], bwpm, 4)
+        transposes(bwT[:], bwpm)
+        permute_x(*X_LOADS[2])
+        for r in range(UNITS[0]):
+            base(0, r)
 
-        for j0, j1 in X_LOADS[1:]:
-            x_group(j0, j1)
-
-        def squares(s):
-            c, h = divmod(s, 2)
-            w = CHUNKS[c] * P
-            xs = xT[:, STARTS[c] * P : STARTS[c] * P + w]
-            sq = sqp.tile([P, 4, w], F32, tag="sq")
-            for t in range(4):
-                g = 4 * h + t
-                who = owner(c, h, t)
-                if who == "gpsimd":
-                    nc.gpsimd.tensor_scalar(
-                        out=sq[:, t, :], in0=xs, scalar1=1.0, scalar2=negg[:, g : g + 1],
-                        op0=ALU.mult, op1=ALU.add,
-                    )
-                    for k in range(0, w, POOL_W):
-                        part = sq[:, t, k : min(k + POOL_W, w)]
-                        nc.gpsimd.tensor_tensor(out=part, in0=part, in1=part, op=ALU.mult)
-                elif who == "vector":
-                    nc.vector.tensor_scalar(
-                        out=sq[:, t, :], in0=xs, scalar1=negg[:, g : g + 1], scalar2=None, op0=ALU.add
-                    )
-                    nc.vector.tensor_tensor(out=sq[:, t, :], in0=sq[:, t, :], in1=sq[:, t, :], op=ALU.mult)
-                else:
-                    nc.scalar.activation(
-                        out=sq[:, t, :], in_=xs, func=ACT.Square, bias=negg[:, g : g + 1], scale=1.0
-                    )
-            return sq
-
-        def exp_quantise(sq, k0, w):
-            grouped = gp.tile([P, w, 4], BF16, tag="grouped", align_bytes=64)
-            nc.scalar.activation(
-                out=grouped[:].rearrange("p (c i) t -> p c t i", i=4),
-                in_=sq[:, :, k0 : k0 + w].rearrange("p t (c i) -> p c t i", i=4),
-                func=ACT.Exp,
-                scale=-20.0,
-            )
-            cd = cp.tile([P, w], U32, tag="codes", align_bytes=64)
-            sc = cp.tile([P, w], U8, tag="scl", align_bytes=64)
-            nc.vector.quantize_mx(
-                out=cd[:].bitcast(FP8X4), scales=sc[:], in_=grouped[:].rearrange("p c t -> p (c t)")
-            )
-            return cd, sc
-
-        def base(c):
-            tiles = []
-            for m in range(0, CHUNKS[c], JRES):
-                n = min(JRES, CHUNKS[c] - m)
-                rt = rp.tile([P, n, OUTS], F32, tag="res")
-                tiles.append(rt)
-                for r in range(n):
-                    j = STARTS[c] + m + r
-                    accb = ps_a.tile([P, OUTS], F32, tag="a")
-                    nc.tensor.matmul(
-                        out=accb[:], lhsT=xT[:, j * P : (j + 1) * P], rhs=bwT[:], start=True, stop=True
-                    )
-                    nc.vector.tensor_copy(out=rt[:, r, :], in_=accb[:])
-            return tiles
-
-        out_view = out.rearrange("(p j) o -> p j o", j=NJ)
-
-        def spline(c, tiles, quantised, m0, nj):
-            for m in range(m0, m0 + nj):
-                rt = tiles[m // JRES]
-                r = m % JRES
-                lo = (m - m0) * P
-                acc = ps_m.tile([P, OUTS], F32, tag="m")
+        for h in range(2):
+            squares_scalar(0, h)
+        for u in range(NU):
+            more = u + 1 < NU
+            groups = new_group(u), new_group(u)
+            codes[u] = new_codes(u), new_codes(u)
+            if u + 2 < NU:
+                transpose_unit(u + 2)
+            if more:
+                differences_vector(u + 1)
                 for h in range(2):
-                    cd, sc = quantised[h]
-                    nc.tensor.matmul_mx(
-                        out=acc[:],
-                        lhsT=cd[:, lo : lo + P].bitcast(FP8X4),
-                        lhsT_scale=sc[:, lo : lo + P],
-                        rhs=wcodes[:, h * OUTS : (h + 1) * OUTS].bitcast(FP8X4),
-                        rhs_scale=wscl[:, h * OUTS : (h + 1) * OUTS],
-                        start=(h == 0),
-                        stop=(h == 1),
-                    )
-                nc.vector.tensor_tensor(out=rt[:, r, :], in0=acc[:], in1=rt[:, r, :], op=ALU.add)
-                n = min(nj, STORE.get((c, m0), JRES))
-                if (m - m0) % n == n - 1:
-                    j = STARTS[c] + m - n + 1
-                    nc.sync.dma_start(out=out_view[:, j : j + n, :], in_=rt[:, r - n + 1 : r + 1, :])
-
-        n_chunks = len(CHUNKS)
-        results = {0: base(0)}
-        sq_tiles = {0: squares(0)}
-        for c in range(n_chunks):
-            if c + 1 < n_chunks:
-                results[c + 1] = base(c + 1)
-            sq_tiles[2 * c + 1] = squares(2 * c + 1)
-            m0 = 0
-            for nj in BLOCKS.get(c, (CHUNKS[c],)):
-                first = exp_quantise(sq_tiles[2 * c], m0 * P, nj * P)
-                if m0 == 0 and c + 1 < n_chunks:
-                    sq_tiles[2 * c + 2] = squares(2 * c + 2)
-                second = exp_quantise(sq_tiles[2 * c + 1], m0 * P, nj * P)
-                spline(c, results[c], (first, second), m0, nj)
-                m0 += nj
+                    exponential(u, h, groups[h], 0, width(u))
+                    squares_scalar(u + 1, h)
+                squares_vector(u + 1)
+                for h in range(2):
+                    quantise(u, h, groups[h], 0, width(u))
+            else:
+                for r0, r1 in END_BLOCKS:
+                    for h in range(2):
+                        exponential(u, h, groups[h], r0 * P, r1 * P)
+                    for h in range(2):
+                        quantise(u, h, groups[h], r0 * P, r1 * P)
+                    for r in range(r0, r1):
+                        spline(u, r)
+                        store(u, r, r + 1)
+                break
+            if u + 2 < NU:
+                gate[u + 2] = gates.tile([P, GRID], F32, tag="gate", name="gate")
+                nc.vector.tensor_copy(out=gate[u + 2][:], in_=negg[:])
+                for h in range(2):
+                    squares_gpsimd(u + 2, h)
+            ahead = list(range(UNITS[u + 1]))
+            for r in range(UNITS[u]):
+                for k in ahead[: len(ahead) // (UNITS[u] - r) + (1 if r == 0 else 0)]:
+                    base(u + 1, k)
+                    ahead.remove(k)
+                spline(u, r)
+                if r % JRES == JRES - 1:
+                    store(u, r - JRES + 1, r + 1)
+            for k in ahead:
+                base(u + 1, k)

@@ -108,24 +108,27 @@ def tile_rbfkanlayer_t_kernel(tc, x, spline_weight, base_weight, grid, out):
         def width(u):
             return UNITS[u] * P
 
-        def x_of(u):
-            return xT[:, FIRST[u] * P : FIRST[u] * P + width(u)]
+        def x_blocks(u, c0=0, c1=None):
+            cols = xT[:, FIRST[u] * P + c0 : FIRST[u] * P + (width(u) if c1 is None else c1)]
+            return cols.rearrange("p (c i) -> p c i", i=4)
+
+        def plane(u, h, t, c0=0, c1=None):
+            return sq_tiles[u, h][:, c0 // 4 : (width(u) if c1 is None else c1) // 4, t, :]
 
         def transpose_unit(u):
             for q in range(FIRST[u] // 4, (FIRST[u] + UNITS[u]) // 4):
                 transpose_x(q)
 
         def squares_gpsimd(u, h):
-            sq_tiles[u, h] = sqp.tile([P, 4, width(u)], F32, tag="sq", name="sq")
+            sq_tiles[u, h] = sqp.tile([P, width(u) // 4, 4, 4], F32, tag="sq", name="sq")
             for t in range(4):
                 if owner(u, h, t) != "gpsimd":
                     continue
                 g = 4 * h + t
-                plane = sq_tiles[u, h][:, t, :]
                 for k in range(0, width(u), POOL_W):
-                    part = plane[:, k : k + POOL_W]
+                    part = plane(u, h, t, k, k + POOL_W)
                     nc.gpsimd.tensor_scalar(
-                        out=part, in0=x_of(u)[:, k : k + POOL_W], scalar1=1.0,
+                        out=part, in0=x_blocks(u, k, k + POOL_W), scalar1=1.0,
                         scalar2=gate.get(u, negg)[:, g : g + 1], op0=ALU.mult, op1=ALU.add,
                     )
                     nc.gpsimd.tensor_tensor(out=part, in0=part, in1=part, op=ALU.mult)
@@ -135,7 +138,7 @@ def tile_rbfkanlayer_t_kernel(tc, x, spline_weight, base_weight, grid, out):
                 if owner(u, h, t) == "scalar":
                     g = 4 * h + t
                     nc.scalar.activation(
-                        out=sq_tiles[u, h][:, t, :], in_=x_of(u), func=ACT.Square, bias=negg[:, g : g + 1], scale=1.0
+                        out=plane(u, h, t), in_=x_blocks(u), func=ACT.Square, bias=negg[:, g : g + 1], scale=1.0
                     )
 
         def vector_planes(u):
@@ -145,13 +148,13 @@ def tile_rbfkanlayer_t_kernel(tc, x, spline_weight, base_weight, grid, out):
             for h, t in vector_planes(u):
                 g = 4 * h + t
                 nc.vector.tensor_scalar(
-                    out=sq_tiles[u, h][:, t, :], in0=x_of(u), scalar1=negg[:, g : g + 1], scalar2=None, op0=ALU.add
+                    out=plane(u, h, t), in0=x_blocks(u), scalar1=negg[:, g : g + 1], scalar2=None, op0=ALU.add
                 )
 
         def squares_vector(u):
             for h, t in vector_planes(u):
-                plane = sq_tiles[u, h][:, t, :]
-                nc.vector.tensor_tensor(out=plane, in0=plane, in1=plane, op=ALU.mult)
+                sq = plane(u, h, t)
+                nc.vector.tensor_tensor(out=sq, in0=sq, in1=sq, op=ALU.mult)
 
         def new_group(u):
             return gp.tile([P, width(u), 4], BF16, tag="grouped", name="grouped", align_bytes=64)
@@ -159,7 +162,7 @@ def tile_rbfkanlayer_t_kernel(tc, x, spline_weight, base_weight, grid, out):
         def exponential(u, h, grouped, c0, c1):
             nc.scalar.activation(
                 out=grouped[:, c0:c1, :].rearrange("p (c i) t -> p c t i", i=4),
-                in_=sq_tiles[u, h][:, :, c0:c1].rearrange("p t (c i) -> p c t i", i=4),
+                in_=sq_tiles[u, h][:, c0 // 4 : c1 // 4, :, :],
                 func=ACT.Exp,
                 scale=-20.0,
             )

@@ -29,9 +29,9 @@ END_BLOCKS = ((0, 2), (2, 4))
 
 
 def owner(u, h, t):
-    if t < (h if u == 0 else 2 if h == 0 and u % 2 else 1):
+    if t == 0 and (u > 0 or h == 1):
         return "gpsimd"
-    if t == 3 and h == 1 and u % 2 == 0:
+    if t == 3 and h == 1 and u != 1 and u < 8:
         return "vector"
     return "scalar"
 
@@ -125,12 +125,12 @@ def tile_rbfkanlayer_t_kernel(tc, x, spline_weight, base_weight, grid, out):
                 if owner(u, h, t) != "gpsimd":
                     continue
                 g = 4 * h + t
+                nc.gpsimd.tensor_scalar(
+                    out=plane(u, h, t), in0=x_blocks(u), scalar1=1.0,
+                    scalar2=gate.get(u, negg)[:, g : g + 1], op0=ALU.mult, op1=ALU.add,
+                )
                 for k in range(0, width(u), POOL_W):
                     part = plane(u, h, t, k, k + POOL_W)
-                    nc.gpsimd.tensor_scalar(
-                        out=part, in0=x_blocks(u, k, k + POOL_W), scalar1=1.0,
-                        scalar2=gate.get(u, negg)[:, g : g + 1], op0=ALU.mult, op1=ALU.add,
-                    )
                     nc.gpsimd.tensor_tensor(out=part, in0=part, in1=part, op=ALU.mult)
 
         def squares_scalar(u, h):

@@ -31,7 +31,7 @@ END_BLOCKS = ((0, 2), (2, 4))
 def owner(u, h, t):
     if t == 0 and (u > 0 or h == 1):
         return "gpsimd"
-    if t == 3 and h == 1 and u != 1 and u < 8:
+    if t == 3 and h == 1 and u in (0, 2, 4, 5, 6):
         return "vector"
     return "scalar"
 
@@ -88,9 +88,9 @@ def tile_rbfkanlayer_t_kernel(tc, x, spline_weight, base_weight, grid, out):
             for q in range(4):
                 nc.vector.tensor_copy(out=dst_w[:, z0:z1, q, :, :], in_=src_w[:, z0:z1, :, q, :])
 
-        def transposes(dst, src):
-            pt = ps_a.tile([P, 4 * P], BF16, tag="a")
-            for r in range(4):
+        def transposes(dst, src, n=4):
+            pt = ps_a.tile([P, n * P], BF16, tag="a")
+            for r in range(n):
                 nc.tensor.transpose(pt[:, r * P : (r + 1) * P], src[:, r * P : (r + 1) * P], ident[:])
             nc.vector.tensor_copy(out=dst, in_=pt[:])
 
@@ -100,10 +100,10 @@ def tile_rbfkanlayer_t_kernel(tc, x, spline_weight, base_weight, grid, out):
         def permute_x(j0, j1):
             permute(xpm, xin, j0, j1)
 
-        def transpose_x(q):
-            transposes(xT[:, 4 * q * P : 4 * (q + 1) * P], xpm[:, 4 * q * P : 4 * (q + 1) * P])
+        def transpose_x(j0, n):
+            transposes(xT[:, j0 * P : (j0 + n) * P], xpm[:, j0 * P : (j0 + n) * P], n)
 
-        sq_tiles, codes, results, gate = {}, {}, {}, {}
+        sq_tiles, codes, results, gate, late = {}, {}, {}, {}, {}
 
         def width(u):
             return UNITS[u] * P
@@ -116,8 +116,7 @@ def tile_rbfkanlayer_t_kernel(tc, x, spline_weight, base_weight, grid, out):
             return sq_tiles[u, h][:, c0 // 4 : (width(u) if c1 is None else c1) // 4, t, :]
 
         def transpose_unit(u):
-            for q in range(FIRST[u] // 4, (FIRST[u] + UNITS[u]) // 4):
-                transpose_x(q)
+            transpose_x(FIRST[u], UNITS[u])
 
         def squares_gpsimd(u, h):
             sq_tiles[u, h] = sqp.tile([P, width(u) // 4, 4, 4], F32, tag="sq", name="sq")
@@ -185,7 +184,10 @@ def tile_rbfkanlayer_t_kernel(tc, x, spline_weight, base_weight, grid, out):
             j = FIRST[u] + r
             accb = ps_a.tile([P, OUTS], F32, tag="a")
             nc.tensor.matmul(out=accb[:], lhsT=xT[:, j * P : (j + 1) * P], rhs=bwT[:], start=True, stop=True)
-            nc.vector.tensor_copy(out=results[u, r // JRES][:, r % JRES, :], in_=accb[:])
+            if u == NU - 1:
+                late[r] = accb
+            else:
+                nc.vector.tensor_copy(out=results[u, r // JRES][:, r % JRES, :], in_=accb[:])
 
         out_view = out.rearrange("(p j) o -> p j o", j=NJ)
 
@@ -260,6 +262,8 @@ def tile_rbfkanlayer_t_kernel(tc, x, spline_weight, base_weight, grid, out):
                 for r0, r1 in END_BLOCKS:
                     for h in range(2):
                         exponential(u, h, groups[h], r0 * P, r1 * P)
+                    for r in range(r0, r1):
+                        nc.scalar.copy(out=results[u, 0][:, r, :], in_=late[r][:])
                     for h in range(2):
                         quantise(u, h, groups[h], r0 * P, r1 * P)
                     for r in range(r0, r1):

@@ -18,20 +18,20 @@ OUTS = 512
 GRID = 8
 NJ = BATCH // P
 JRES = 4
-UNITS = (4, 8, 8, 8, 8, 8, 8, 4, 4, 4)
+UNITS = (4, 8, 8, 8, 8, 8, 8, 4, 8)
 NU = len(UNITS)
 FIRST = tuple(sum(UNITS[:u]) for u in range(NU))
 FLOPS = 2 * BATCH * (FEAT * GRID) * OUTS + 2 * BATCH * FEAT * OUTS
 
 X_LOADS = ((0, 4), (4, 16), (16, 64))
 POOL_W = 512
-END_BLOCKS = ((0, 2), (2, 4))
+END_BLOCKS = ((0, 4), (4, 8))
 
 
 def owner(u, h, t):
     if t == 0 and (u > 0 or h == 1):
         return "gpsimd"
-    if t == 3 and h == 1 and u in (0, 2, 4, 5, 6):
+    if t == 3 and h == 1 and u in (0, 2, 3, 4, 5, 6):
         return "vector"
     return "scalar"
 
@@ -184,7 +184,7 @@ def tile_rbfkanlayer_t_kernel(tc, x, spline_weight, base_weight, grid, out):
             j = FIRST[u] + r
             accb = ps_a.tile([P, OUTS], F32, tag="a")
             nc.tensor.matmul(out=accb[:], lhsT=xT[:, j * P : (j + 1) * P], rhs=bwT[:], start=True, stop=True)
-            if u == NU - 1:
+            if u == NU - 1 and r >= 4:
                 late[r] = accb
             else:
                 nc.vector.tensor_copy(out=results[u, r // JRES][:, r % JRES, :], in_=accb[:])
@@ -248,10 +248,11 @@ def tile_rbfkanlayer_t_kernel(tc, x, spline_weight, base_weight, grid, out):
             more = u + 1 < NU
             groups = new_group(u), new_group(u)
             codes[u] = new_codes(u), new_codes(u)
+            if more:
+                differences_vector(u + 1)
             if u + 2 < NU:
                 transpose_unit(u + 2)
             if more:
-                differences_vector(u + 1)
                 for h in range(2):
                     exponential(u, h, groups[h], 0, width(u))
                     squares_scalar(u + 1, h)
@@ -263,7 +264,8 @@ def tile_rbfkanlayer_t_kernel(tc, x, spline_weight, base_weight, grid, out):
                     for h in range(2):
                         exponential(u, h, groups[h], r0 * P, r1 * P)
                     for r in range(r0, r1):
-                        nc.scalar.copy(out=results[u, 0][:, r, :], in_=late[r][:])
+                        if r in late:
+                            nc.scalar.copy(out=results[u, r // JRES][:, r % JRES, :], in_=late[r][:])
                     for h in range(2):
                         quantise(u, h, groups[h], r0 * P, r1 * P)
                     for r in range(r0, r1):

from contextlib import ExitStack

import concourse.mybir as mybir
from concourse.masks import make_identity

F32 = mybir.dt.float32
BF16 = mybir.dt.bfloat16
U32 = mybir.dt.uint32
U8 = mybir.dt.uint8
FP8X4 = mybir.dt.float8_e4m3fn_x4
ACT = mybir.ActivationFunctionType
ALU = mybir.AluOpType

P = 128
BATCH = 8192
FEAT = 128
OUTS = 512
GRID = 8
NJ = BATCH // P
JRES = 4
UNITS = (4, 8, 8, 8, 8, 8, 8, 4, 8)
NU = len(UNITS)
FIRST = tuple(sum(UNITS[:u]) for u in range(NU))
FLOPS = 2 * BATCH * (FEAT * GRID) * OUTS + 2 * BATCH * FEAT * OUTS

X_LOADS = ((0, 4), (4, 16), (16, 64))
POOL_W = 512
END_BLOCKS = ((0, 4), (4, 8))


def owner(u, h, t):
    if t == 0 and (u > 0 or h == 1):
        return "gpsimd"
    if t == 3 and h == 1 and u in (0, 2, 3, 4, 5, 6):
        return "vector"
    return "scalar"


def tile_rbfkanlayer_t_kernel(tc, x, spline_weight, base_weight, grid, out):
    nc = tc.nc
    with ExitStack() as stack:
        stack.enter_context(tc.manual_schedule())
        keep = stack.enter_context(tc.tile_pool(name="keep", bufs=1))
        sqp = stack.enter_context(tc.tile_pool(name="sqp", bufs=4))
        gates = stack.enter_context(tc.tile_pool(name="gates", bufs=2))
        gp = stack.enter_context(tc.tile_pool(name="gp", bufs=3))
        cp = stack.enter_context(tc.tile_pool(name="cp", bufs=4))
        rp = stack.enter_context(tc.tile_pool(name="rp", bufs=6))
        ps_a = stack.enter_context(tc.psum_pool(name="ps_a", bufs=4))
        ps_m = stack.enter_context(tc.psum_pool(name="ps_m", bufs=4))

        gb = keep.tile([P, GRID], BF16)
        nc.scalar.dma_start(out=gb[:], in_=grid.partition_broadcast(P))
        xin = keep.tile([P, NJ * FEAT], BF16)
        x_view = x.rearrange("(p j) i -> p (j i)", j=NJ)

        def load_x(j0, j1):
            nc.sync.dma_start(out=xin[:, j0 * FEAT : j1 * FEAT], in_=x_view[:, j0 * FEAT : j1 * FEAT])

        load_x(*X_LOADS[0])
        load_x(*X_LOADS[1])
        wraw = keep.tile([P, GRID, OUTS], BF16)
        w_view = spline_weight.rearrange("(n q e g) o -> q e n (g o)", n=8, q=4, e=4)
        for q in range(4):
            for e in range(4):
                p0 = 32 * q + e
                nc.sync.dma_start(
                    out=wraw[p0 : p0 + 29 : 4, :, :].rearrange("p g o -> p (g o)"), in_=w_view[q, e, :, :]
                )
        bwin = keep.tile([P, 4 * FEAT], BF16)
        nc.sync.dma_start(
            out=bwin[:].rearrange("p (t i) -> p t i", t=4),
            in_=base_weight.rearrange("(t p) i -> p t i", p=P),
        )
        load_x(*X_LOADS[2])

        warm = keep.tile([P, 2], F32)
        nc.vector.memset(warm[:], 0.0)
        nc.scalar.activation(out=warm[:, 1:2], in_=warm[:, 0:1], func=ACT.Exp)
        ident = keep.tile([P, P], BF16)
        make_identity(nc, ident[:])
        negg = keep.tile([P, GRID], F32)
        nc.vector.tensor_scalar(out=negg[:], in0=gb[:], scalar1=-1.0, scalar2=None, op0=ALU.mult)

        def permute(dst, src, z0, z1):
            dst_w = dst[:].bitcast(F32).rearrange("p (z q n w) -> p z q n w", q=4, n=8, w=2)
            src_w = src[:].bitcast(F32).rearrange("p (z n q w) -> p z n q w", q=4, n=8, w=2)
            for q in range(4):
                nc.vector.tensor_copy(out=dst_w[:, z0:z1, q, :, :], in_=src_w[:, z0:z1, :, q, :])

        def transposes(dst, src, n=4):
            pt = ps_a.tile([P, n * P], BF16, tag="a")
            for r in range(n):
                nc.tensor.transpose(pt[:, r * P : (r + 1) * P], src[:, r * P : (r + 1) * P], ident[:])
            nc.vector.tensor_copy(out=dst, in_=pt[:])

        xpm = keep.tile([P, NJ * FEAT], BF16)
        xT = keep.tile([P, BATCH], BF16)

        def permute_x(j0, j1):
            permute(xpm, xin, j0, j1)

        def transpose_x(j0, n):
            transposes(xT[:, j0 * P : (j0 + n) * P], xpm[:, j0 * P : (j0 + n) * P], n)

        sq_tiles, codes, results, gate, late = {}, {}, {}, {}, {}

        def width(u):
            return UNITS[u] * P

        def x_blocks(u, c0=0, c1=None):
            cols = xT[:, FIRST[u] * P + c0 : FIRST[u] * P + (width(u) if c1 is None else c1)]
            return cols.rearrange("p (c i) -> p c i", i=4)

        def plane(u, h, t, c0=0, c1=None):
            return sq_tiles[u, h][:, c0 // 4 : (width(u) if c1 is None else c1) // 4, t, :]

        def transpose_unit(u):
            transpose_x(FIRST[u], UNITS[u])

        def squares_gpsimd(u, h):
            sq_tiles[u, h] = sqp.tile([P, width(u) // 4, 4, 4], F32, tag="sq", name="sq")
            for t in range(4):
                if owner(u, h, t) != "gpsimd":
                    continue
                g = 4 * h + t
                nc.gpsimd.tensor_scalar(
                    out=plane(u, h, t), in0=x_blocks(u), scalar1=1.0,
                    scalar2=gate.get(u, negg)[:, g : g + 1], op0=ALU.mult, op1=ALU.add,
                )
                for k in range(0, width(u), POOL_W):
                    part = plane(u, h, t, k, k + POOL_W)
                    nc.gpsimd.tensor_tensor(out=part, in0=part, in1=part, op=ALU.mult)

        def squares_scalar(u, h):
            for t in range(4):
                if owner(u, h, t) == "scalar":
                    g = 4 * h + t
                    nc.scalar.activation(
                        out=plane(u, h, t), in_=x_blocks(u), func=ACT.Square, bias=negg[:, g : g + 1], scale=1.0
                    )

        def vector_planes(u):
            return [(h, t) for h in range(2) for t in range(4) if owner(u, h, t) == "vector"]

        def differences_vector(u):
            for h, t in vector_planes(u):
                g = 4 * h + t
                nc.vector.tensor_scalar(
                    out=plane(u, h, t), in0=x_blocks(u), scalar1=negg[:, g : g + 1], scalar2=None, op0=ALU.add
                )

        def squares_vector(u):
            for h, t in vector_planes(u):
                sq = plane(u, h, t)
                nc.vector.tensor_tensor(out=sq, in0=sq, in1=sq, op=ALU.mult)

        def new_group(u):
            return gp.tile([P, width(u), 4], BF16, tag="grouped", name="grouped", align_bytes=64)

        def exponential(u, h, grouped, c0, c1):
            nc.scalar.activation(
                out=grouped[:, c0:c1, :].rearrange("p (c i) t -> p c t i", i=4),
                in_=sq_tiles[u, h][:, c0 // 4 : c1 // 4, :, :],
                func=ACT.Exp,
                scale=-20.0,
            )

        def new_codes(u):
            cd = cp.tile([P, width(u)], U32, tag="codes", align_bytes=64)
            sc = cp.tile([P, width(u)], U8, tag="scl", align_bytes=64)
            return cd, sc

        def quantise(u, h, grouped, c0, c1):
            cd, sc = codes[u][h]
            nc.vector.quantize_mx(
                out=cd[:, c0:c1].bitcast(FP8X4), scales=sc[:, c0:c1],
                in_=grouped[:, c0:c1, :].rearrange("p c t -> p (c t)"),
            )

        def base(u, r):
            if r % JRES == 0:
                results[u, r // JRES] = rp.tile([P, JRES, OUTS], F32, tag="res", name="res")
            j = FIRST[u] + r
            accb = ps_a.tile([P, OUTS], F32, tag="a")
            nc.tensor.matmul(out=accb[:], lhsT=xT[:, j * P : (j + 1) * P], rhs=bwT[:], start=True, stop=True)
            if u == NU - 1 and r >= 4:
                late[r] = accb
            else:
                nc.vector.tensor_copy(out=results[u, r // JRES][:, r % JRES, :], in_=accb[:])

        out_view = out.rearrange("(p j) o -> p j o", j=NJ)

        def spline(u, r):
            rt = results[u, r // JRES]
            acc = ps_m.tile([P, OUTS], F32, tag="m")
            for h, (cd, sc) in enumerate(codes[u]):
                nc.tensor.matmul_mx(
                    out=acc[:],
                    lhsT=cd[:, r * P : (r + 1) * P].bitcast(FP8X4),
                    lhsT_scale=sc[:, r * P : (r + 1) * P],
                    rhs=wcodes[:, h * OUTS : (h + 1) * OUTS].bitcast(FP8X4),
                    rhs_scale=wscl[:, h * OUTS : (h + 1) * OUTS],
                    start=(h == 0),
                    stop=(h == 1),
                )
            nc.vector.tensor_tensor(out=rt[:, r % JRES, :], in0=acc[:], in1=rt[:, r % JRES, :], op=ALU.add)

        def store(u, r0, r1):
            j = FIRST[u]
            nc.sync.dma_start(
                out=out_view[:, j + r0 : j + r1, :], in_=results[u, r0 // JRES][:, r0 % JRES : r0 % JRES + r1 - r0, :]
            )

        permute_x(*X_LOADS[0])
        transpose_unit(0)
        permute_x(*X_LOADS[1])
        transpose_unit(1)
        for h in range(2):
            squares_gpsimd(0, h)
        differences_vector(0)
        squares_vector(0)
        for h in range(2):
            squares_gpsimd(1, h)

        wgrp = keep.tile([P, 2, OUTS, 4], BF16, align_bytes=64)
        for h in range(2):
            nc.vector.tensor_copy(
                out=wgrp[:, h, :, :].rearrange("p (c i) t -> p c t i", i=4),
                in_=wraw[:, 4 * h : 4 * h + 4, :].rearrange("p t (c i) -> p c t i", i=4),
            )
        wcodes = keep.tile([P, 2 * OUTS], U32, align_bytes=64)
        wscl = keep.tile([P, 2 * OUTS], U8, align_bytes=64)
        nc.vector.quantize_mx(
            out=wcodes[:].bitcast(FP8X4), scales=wscl[:], in_=wgrp[:].rearrange("p h o t -> p (h o t)")
        )
        bwpm = keep.tile([P, 4 * FEAT], BF16)
        permute(bwpm, bwin, 0, 4)
        bwT = keep.tile([P, OUTS], BF16)
        transposes(bwT[:], bwpm)
        permute_x(*X_LOADS[2])
        for r in range(UNITS[0]):
            base(0, r)

        for h in range(2):
            squares_scalar(0, h)
        for u in range(NU):
            more = u + 1 < NU
            groups = new_group(u), new_group(u)
            codes[u] = new_codes(u), new_codes(u)
            if more:
                differences_vector(u + 1)
            if u + 2 < NU:
                transpose_unit(u + 2)
            if more:
                for h in range(2):
                    exponential(u, h, groups[h], 0, width(u))
                    squares_scalar(u + 1, h)
                squares_vector(u + 1)
                for h in range(2):
                    quantise(u, h, groups[h], 0, width(u))
            else:
                for r0, r1 in END_BLOCKS:
                    for h in range(2):
                        exponential(u, h, groups[h], r0 * P, r1 * P)
                    for r in range(r0, r1):
                        if r in late:
                            nc.scalar.copy(out=results[u, r // JRES][:, r % JRES, :], in_=late[r][:])
                    for h in range(2):
                        quantise(u, h, groups[h], r0 * P, r1 * P)
                    for r in range(r0, r1):
                        spline(u, r)
                        store(u, r, r + 1)
                break
            if u + 2 < NU:
                gate[u + 2] = gates.tile([P, GRID], F32, tag="gate", name="gate")
                nc.vector.tensor_copy(out=gate[u + 2][:], in_=negg[:])
                for h in range(2):
                    squares_gpsimd(u + 2, h)
            ahead = list(range(UNITS[u + 1]))
            for r in range(UNITS[u]):
                for k in ahead[: len(ahead) // (UNITS[u] - r) + (1 if r == 0 else 0)]:
                    base(u + 1, k)
                    ahead.remove(k)
                spline(u, r)
                if r % JRES == JRES - 1:
                    store(u, r - JRES + 1, r + 1)
            for k in ahead:
                base(u + 1, k)
